import numpy as np
import ml_dtypes


def mxq(x, axis, fmt="e4m3"):
    dtype, down = {"e4m3": (ml_dtypes.float8_e4m3fn, 7), "e5m2": (ml_dtypes.float8_e5m2, 14)}[fmt]
    v = np.moveaxis(np.asarray(x, np.float32).astype(ml_dtypes.bfloat16).astype(np.float64), axis, -1)
    blocks = v.reshape(v.shape[:-1] + (-1, 32))
    amax = np.abs(blocks).max(-1, keepdims=True)
    byte = np.maximum(np.where(amax > 0, np.frexp(amax)[1] - 1 + 127, 0) - down, 1)
    scale = np.exp2(byte - 127.0)
    codes = (blocks / scale).astype(np.float32).astype(dtype).astype(np.float64)
    return np.moveaxis((codes * scale).reshape(v.shape), -1, axis)


WIDE = False


def mx_kscale(k):
    if not WIDE:
        return np.ones(k)
    levels = np.array([10, -10, 5, -5, 0])
    a = np.random.permutation(np.resize(levels, k // 512 * 4)).reshape(k // 512, 4)
    idx = np.arange(k)
    return np.exp2(a[idx // 512, idx % 128 // 32])


BF16 = ml_dtypes.bfloat16


def bf(x):
    return np.asarray(x, np.float32).astype(BF16)


def f64(x):
    return np.asarray(x).astype(np.float64)


E, D_NODE, D_EDGE, D_GLOB, LATENT, D_OUT = 4096, 128, 128, 128, 512, 128
D_IN = D_NODE + D_NODE + D_EDGE + D_GLOB


def setup_inputs():
    s = mx_kscale(D_IN)
    o1 = D_NODE
    o2 = o1 + D_NODE
    o3 = o2 + D_EDGE
    return {
        "receiver": bf(np.random.standard_normal((E, D_NODE)) * s[:o1]),
        "sender": bf(np.random.standard_normal((E, D_NODE)) * s[o1:o2]),
        "edge_attr": bf(np.random.standard_normal((E, D_EDGE)) * s[o2:o3]),
        "global_attr": bf(np.random.standard_normal((1, D_GLOB)) * s[o3:]),
        "W1": bf(np.random.standard_normal((D_IN, LATENT)) / np.sqrt(D_IN) / s[:, None]),
        "b1": bf(np.random.standard_normal(LATENT) * 0.1),
    }


def reference(receiver, sender, edge_attr, global_attr, W1, b1):
    e = edge_attr.shape[0]
    g = np.tile(f64(global_attr), (e // global_attr.shape[0], 1))
    x = np.concatenate([f64(receiver), f64(sender), f64(edge_attr), g], axis=1)
    return np.maximum((mxq(x, 1, "e4m3") @ mxq(f64(W1), 0, "e4m3")) + f64(b1), 0.0)

@@ -1,0 +1,170 @@
+from contextlib import ExitStack
+
+import concourse.masks as masks
+import concourse.mybir as mybir
+
+FP8X4 = mybir.dt.float8_e4m3fn_x4
+BF16 = mybir.dt.bfloat16
+F32 = mybir.dt.float32
+U32 = mybir.dt.uint32
+U8 = mybir.dt.uint8
+
+P = 128
+PACK = 4
+EDGES = 4096
+D_PIECE = 128
+PIECES_PER_EDGE = 3
+LATENT = 512
+SETS = EDGES // P
+GROUP_SETS = 2
+GROUP_EDGES = GROUP_SETS * P
+GROUPS = SETS // GROUP_SETS
+GROUPED_TILES = 2
+RELU_ON_VECTOR_EVERY = 4
+
+FLOPS = 2 * EDGES * (PACK * D_PIECE) * LATENT
+
+
+def load_chunks():
+    chunks = []
+    first = 0
+    width = GROUP_SETS
+    while first < SETS:
+        chunks.append((first, width))
+        first += width
+        width = first
+    return chunks
+
+
+def tile_edgemodel_pa_kernel(tc, receiver, sender, edge_attr, global_attr, W1, b1, out):
+    nc = tc.nc
+    with ExitStack() as ctx:
+        ctx.enter_context(tc.manual_schedule())
+        consts = ctx.enter_context(tc.tile_pool(name="consts", bufs=1))
+        x_pool = ctx.enter_context(tc.tile_pool(name="x", bufs=1))
+        mx_pool = ctx.enter_context(tc.tile_pool(name="mx", bufs=3))
+        y_pool = ctx.enter_context(tc.tile_pool(name="y", bufs=6))
+        psum_t = ctx.enter_context(tc.psum_pool(name="psum_t", bufs=3))
+        psum_acc = ctx.enter_context(tc.psum_pool(name="psum_acc", bufs=5))
+
+        g_rows = consts.tile([P, D_PIECE], BF16)
+        nc.vector.memset(g_rows[:], 0.0)
+        nc.scalar.dma_start(out=g_rows[0:1, :], in_=global_attr)
+        b_rows = consts.tile([P, LATENT], BF16)
+        nc.vector.memset(b_rows[:], 0.0)
+        nc.scalar.dma_start(out=b_rows[0:1, :], in_=b1.rearrange("(o n) -> o n", o=1))
+        ones = consts.tile([P, P], BF16)
+        nc.vector.memset(ones[:], 1.0)
+        ident = consts.tile([P, P], BF16)
+        masks.make_identity(nc, ident[:])
+
+        w_raw = consts.tile([P, PACK, LATENT], BF16)
+        nc.sync.dma_start(out=w_raw[:], in_=W1.rearrange("(f p) n -> p f n", p=P))
+
+        x_of_set = {}
+        for first, width in load_chunks():
+            for piece, source in enumerate((receiver, sender, edge_attr)):
+                chunk = x_pool.tile([P, width, D_PIECE], BF16, name="x%d_%d" % (piece, first))
+                by_set = source.rearrange("(p t) d -> p t d", t=SETS)
+                nc.sync.dma_start(out=chunk[:], in_=by_set[:, first : first + width, :])
+                for k in range(width):
+                    x_of_set[(piece, first + k)] = chunk[:, k, :]
+
+        g_ps = psum_t.tile([P, PIECES_PER_EDGE, GROUP_EDGES], BF16, name="xt")
+        nc.tensor.transpose(g_ps[:, 0, 0:P], g_rows[:], ident[:])
+        grouped_tiles = []
+        for n in range(GROUPED_TILES):
+            grouped = consts.tile([P, GROUP_EDGES, PACK], BF16, name="grouped%d" % n, align_bytes=64)
+            nc.scalar.copy(out=grouped[:, :, 3], in_=g_ps[:, 0, 0:1].to_broadcast([P, GROUP_EDGES]))
+            grouped_tiles.append(grouped)
+
+        bias_ps = psum_acc.tile([P, LATENT], F32, name="acc")
+        nc.tensor.matmul(out=bias_ps[:], lhsT=ones[:], rhs=b_rows[:], start=True, stop=True)
+        bias_all = consts.tile([P, LATENT], F32)
+
+        w_grouped = consts.tile([P, LATENT, PACK], BF16, align_bytes=64)
+        nc.vector.tensor_copy(out=w_grouped[:], in_=w_raw[:].rearrange("p f n -> p n f"))
+        nc.vector.tensor_copy(out=bias_all[:], in_=bias_ps[:])
+        w_codes = consts.tile([P, LATENT], U32, align_bytes=64)
+        w_scales = consts.tile([P, LATENT], U8, align_bytes=64)
+        nc.vector.quantize_mx(
+            out=w_codes[:].bitcast(FP8X4),
+            scales=w_scales[:],
+            in_=w_grouped[:].rearrange("p n f -> p (n f)"),
+        )
+
+        out_by_set = out.rearrange("(p t) n -> p t n", t=SETS)
+        xt_of = {}
+        codes_of = {}
+        acc_of = {}
+        y_of = {}
+
+        def transpose(i):
+            xt = psum_t.tile([P, PIECES_PER_EDGE, GROUP_EDGES], BF16, name="xt")
+            for j in range(GROUP_SETS):
+                for piece in range(PIECES_PER_EDGE):
+                    nc.tensor.transpose(
+                        xt[:, piece, j * P : (j + 1) * P],
+                        x_of_set[(piece, i * GROUP_SETS + j)],
+                        ident[:],
+                    )
+            xt_of[i] = xt
+
+        def regroup(i):
+            grouped = grouped_tiles[i % GROUPED_TILES]
+            nc.scalar.copy(
+                out=grouped[:, :, 0:PIECES_PER_EDGE],
+                in_=xt_of[i][:].rearrange("p piece e -> p e piece"),
+            )
+
+        def quantise(i):
+            codes = mx_pool.tile([P, GROUP_EDGES], U32, name="x_codes", align_bytes=64)
+            scales = mx_pool.tile([P, GROUP_EDGES], U8, name="x_scales", align_bytes=64)
+            nc.vector.quantize_mx(
+                out=codes[:].bitcast(FP8X4),
+                scales=scales[:],
+                in_=grouped_tiles[i % GROUPED_TILES][:].rearrange("p e f -> p (e f)"),
+            )
+            codes_of[i] = (codes, scales)
+
+        def multiply(i):
+            codes, scales = codes_of[i]
+            for j in range(GROUP_SETS):
+                edges = slice(j * P, (j + 1) * P)
+                acc = psum_acc.tile([P, LATENT], F32, name="acc")
+                nc.tensor.matmul_mx(
+                    out=acc[:],
+                    lhsT=codes[:, edges].bitcast(FP8X4),
+                    lhsT_scale=scales[:, edges],
+                    rhs=w_codes[:].bitcast(FP8X4),
+                    rhs_scale=w_scales[:],
+                    start=True,
+                    stop=True,
+                )
+                acc_of[(i, j)] = acc
+
+        def add_bias(i):
+            y = y_pool.tile([P, GROUP_SETS, LATENT], F32, name="y")
+            for j in range(GROUP_SETS):
+                nc.vector.tensor_tensor(
+                    out=y[:, j, :], in0=acc_of[(i, j)][:], in1=bias_all[:], op=mybir.AluOpType.add
+                )
+            y_of[i] = y
+
+        def relu_and_store(i):
+            y = y_of[i]
+            flat = y[:].rearrange("p j n -> p (j n)")
+            if i % RELU_ON_VECTOR_EVERY == RELU_ON_VECTOR_EVERY - 1:
+                nc.vector.tensor_scalar_max(out=flat, in0=flat, scalar1=0.0)
+            else:
+                nc.scalar.activation(out=flat, in_=flat, func=mybir.ActivationFunctionType.Relu)
+            nc.sync.dma_start(
+                out=out_by_set[:, i * GROUP_SETS : (i + 1) * GROUP_SETS, :], in_=y[:]
+            )
+
+        stages = (transpose, regroup, quantise, multiply, add_bias, relu_and_store)
+        for step in range(GROUPS + len(stages) - 1):
+            for lag, stage in enumerate(stages):
+                i = step - lag
+                if 0 <= i < GROUPS:
+                    stage(i)

@@ -20,7 +20,6 @@ GROUP_SETS = 2
 GROUP_EDGES = GROUP_SETS * P
 GROUPS = SETS // GROUP_SETS
 GROUPED_TILES = 2
-RELU_ON_VECTOR_EVERY = 4
 
 FLOPS = 2 * EDGES * (PACK * D_PIECE) * LATENT
 
@@ -153,11 +152,17 @@ def tile_edgemodel_pa_kernel(tc, receiver, sender, edge_attr, global_attr, W1, b
 
         def relu_and_store(i):
             y = y_of[i]
-            flat = y[:].rearrange("p j n -> p (j n)")
-            if i % RELU_ON_VECTOR_EVERY == RELU_ON_VECTOR_EVERY - 1:
-                nc.vector.tensor_scalar_max(out=flat, in0=flat, scalar1=0.0)
-            else:
-                nc.scalar.activation(out=flat, in_=flat, func=mybir.ActivationFunctionType.Relu)
+            nc.scalar.activation(
+                out=y[:, 0, :], in_=y[:, 0, :], func=mybir.ActivationFunctionType.Relu
+            )
+            nc.gpsimd.tensor_scalar(
+                out=y[:, 1, :],
+                in0=y[:, 1, :],
+                scalar1=float("inf"),
+                scalar2=0.0,
+                op0=mybir.AluOpType.min,
+                op1=mybir.AluOpType.max,
+            )
             nc.sync.dma_start(
                 out=out_by_set[:, i * GROUP_SETS : (i + 1) * GROUP_SETS, :], in_=y[:]
             )

@@ -42,7 +42,7 @@ def tile_edgemodel_pa_kernel(tc, receiver, sender, edge_attr, global_attr, W1, b
         consts = ctx.enter_context(tc.tile_pool(name="consts", bufs=1))
         x_pool = ctx.enter_context(tc.tile_pool(name="x", bufs=1))
         mx_pool = ctx.enter_context(tc.tile_pool(name="mx", bufs=3))
-        y_pool = ctx.enter_context(tc.tile_pool(name="y", bufs=6))
+        y_pool = ctx.enter_context(tc.tile_pool(name="y", bufs=12))
         psum_t = ctx.enter_context(tc.psum_pool(name="psum_t", bufs=3))
         psum_acc = ctx.enter_context(tc.psum_pool(name="psum_acc", bufs=5))
 
@@ -56,6 +56,10 @@ def tile_edgemodel_pa_kernel(tc, receiver, sender, edge_attr, global_attr, W1, b
         nc.vector.memset(ones[:], 1.0)
         ident = consts.tile([P, P], BF16)
         masks.make_identity(nc, ident[:])
+        table_warmer = consts.tile([P, 1], F32)
+        nc.scalar.activation(
+            out=table_warmer[:], in_=ones[:, 0:1], func=mybir.ActivationFunctionType.Relu
+        )
 
         w_raw = consts.tile([P, PACK, LATENT], BF16)
         nc.sync.dma_start(out=w_raw[:], in_=W1.rearrange("(f p) n -> p f n", p=P))
@@ -80,17 +84,22 @@ def tile_edgemodel_pa_kernel(tc, receiver, sender, edge_attr, global_attr, W1, b
         bias_ps = psum_acc.tile([P, LATENT], F32, name="acc")
         nc.tensor.matmul(out=bias_ps[:], lhsT=ones[:], rhs=b_rows[:], start=True, stop=True)
         bias_all = consts.tile([P, LATENT], F32)
+        nc.vector.tensor_copy(out=bias_all[:], in_=bias_ps[:])
 
         w_grouped = consts.tile([P, LATENT, PACK], BF16, align_bytes=64)
-        nc.vector.tensor_copy(out=w_grouped[:], in_=w_raw[:].rearrange("p f n -> p n f"))
-        nc.vector.tensor_copy(out=bias_all[:], in_=bias_ps[:])
         w_codes = consts.tile([P, LATENT], U32, align_bytes=64)
         w_scales = consts.tile([P, LATENT], U8, align_bytes=64)
-        nc.vector.quantize_mx(
-            out=w_codes[:].bitcast(FP8X4),
-            scales=w_scales[:],
-            in_=w_grouped[:].rearrange("p n f -> p (n f)"),
-        )
+        w_halves = (slice(0, LATENT // 2), slice(LATENT // 2, LATENT))
+        for cols in w_halves:
+            nc.vector.tensor_copy(
+                out=w_grouped[:, cols, :], in_=w_raw[:, :, cols].rearrange("p f n -> p n f")
+            )
+        for cols in w_halves:
+            nc.vector.quantize_mx(
+                out=w_codes[:, cols].bitcast(FP8X4),
+                scales=w_scales[:, cols],
+                in_=w_grouped[:, cols, :].rearrange("p n f -> p (n f)"),
+            )
 
         out_by_set = out.rearrange("(p t) n -> p t n", t=SETS)
         xt_of = {}
@@ -143,29 +152,28 @@ def tile_edgemodel_pa_kernel(tc, receiver, sender, edge_attr, global_attr, W1, b
                 acc_of[(i, j)] = acc
 
         def add_bias(i):
-            y = y_pool.tile([P, GROUP_SETS, LATENT], F32, name="y")
             for j in range(GROUP_SETS):
+                y = y_pool.tile([P, LATENT], F32, name="y")
                 nc.vector.tensor_tensor(
-                    out=y[:, j, :], in0=acc_of[(i, j)][:], in1=bias_all[:], op=mybir.AluOpType.add
+                    out=y[:], in0=acc_of[(i, j)][:], in1=bias_all[:], op=mybir.AluOpType.add
                 )
-            y_of[i] = y
+                y_of[(i, j)] = y
 
         def relu_and_store(i):
-            y = y_of[i]
+            y_scalar, y_gpsimd = y_of[(i, 0)], y_of[(i, 1)]
             nc.scalar.activation(
-                out=y[:, 0, :], in_=y[:, 0, :], func=mybir.ActivationFunctionType.Relu
+                out=y_scalar[:], in_=y_scalar[:], func=mybir.ActivationFunctionType.Relu
             )
+            nc.sync.dma_start(out=out_by_set[:, i * GROUP_SETS, :], in_=y_scalar[:])
             nc.gpsimd.tensor_scalar(
-                out=y[:, 1, :],
-                in0=y[:, 1, :],
+                out=y_gpsimd[:],
+                in0=y_gpsimd[:],
                 scalar1=float("inf"),
                 scalar2=0.0,
                 op0=mybir.AluOpType.min,
                 op1=mybir.AluOpType.max,
             )
-            nc.sync.dma_start(
-                out=out_by_set[:, i * GROUP_SETS : (i + 1) * GROUP_SETS, :], in_=y[:]
-            )
+            nc.sync.dma_start(out=out_by_set[:, i * GROUP_SETS + 1, :], in_=y_gpsimd[:])
 
         stages = (transpose, regroup, quantise, multiply, add_bias, relu_and_store)
         for step in range(GROUPS + len(stages) - 1):

@@ -8,6 +8,7 @@ BF16 = mybir.dt.bfloat16
 F32 = mybir.dt.float32
 U32 = mybir.dt.uint32
 U8 = mybir.dt.uint8
+RELU = mybir.ActivationFunctionType.Relu
 
 P = 128
 PACK = 4
@@ -27,7 +28,7 @@ FLOPS = 2 * EDGES * (PACK * D_PIECE) * LATENT
 def load_chunks():
     chunks = []
     first = 0
-    width = GROUP_SETS
+    width = 2 * GROUP_SETS
     while first < SETS:
         chunks.append((first, width))
         first += width
@@ -42,24 +43,18 @@ def tile_edgemodel_pa_kernel(tc, receiver, sender, edge_attr, global_attr, W1, b
         consts = ctx.enter_context(tc.tile_pool(name="consts", bufs=1))
         x_pool = ctx.enter_context(tc.tile_pool(name="x", bufs=1))
         mx_pool = ctx.enter_context(tc.tile_pool(name="mx", bufs=3))
-        y_pool = ctx.enter_context(tc.tile_pool(name="y", bufs=12))
+        y_pool = ctx.enter_context(tc.tile_pool(name="y", bufs=6))
         psum_t = ctx.enter_context(tc.psum_pool(name="psum_t", bufs=3))
         psum_acc = ctx.enter_context(tc.psum_pool(name="psum_acc", bufs=5))
 
         g_rows = consts.tile([P, D_PIECE], BF16)
         nc.vector.memset(g_rows[:], 0.0)
-        nc.scalar.dma_start(out=g_rows[0:1, :], in_=global_attr)
         b_rows = consts.tile([P, LATENT], BF16)
         nc.vector.memset(b_rows[:], 0.0)
-        nc.scalar.dma_start(out=b_rows[0:1, :], in_=b1.rearrange("(o n) -> o n", o=1))
-        ones = consts.tile([P, P], BF16)
+        ones = consts.tile([P, GROUP_EDGES], BF16)
         nc.vector.memset(ones[:], 1.0)
         ident = consts.tile([P, P], BF16)
         masks.make_identity(nc, ident[:])
-        table_warmer = consts.tile([P, 1], F32)
-        nc.scalar.activation(
-            out=table_warmer[:], in_=ones[:, 0:1], func=mybir.ActivationFunctionType.Relu
-        )
 
         w_raw = consts.tile([P, PACK, LATENT], BF16)
         nc.sync.dma_start(out=w_raw[:], in_=W1.rearrange("(f p) n -> p f n", p=P))
@@ -72,19 +67,12 @@ def tile_edgemodel_pa_kernel(tc, receiver, sender, edge_attr, global_attr, W1, b
                 nc.sync.dma_start(out=chunk[:], in_=by_set[:, first : first + width, :])
                 for k in range(width):
                     x_of_set[(piece, first + k)] = chunk[:, k, :]
+            if first == 0:
+                nc.scalar.dma_start(out=g_rows[0:1, :], in_=global_attr)
+                nc.scalar.dma_start(out=b_rows[0:1, :], in_=b1.rearrange("(o n) -> o n", o=1))
 
-        g_ps = psum_t.tile([P, PIECES_PER_EDGE, GROUP_EDGES], BF16, name="xt")
-        nc.tensor.transpose(g_ps[:, 0, 0:P], g_rows[:], ident[:])
-        grouped_tiles = []
-        for n in range(GROUPED_TILES):
-            grouped = consts.tile([P, GROUP_EDGES, PACK], BF16, name="grouped%d" % n, align_bytes=64)
-            nc.scalar.copy(out=grouped[:, :, 3], in_=g_ps[:, 0, 0:1].to_broadcast([P, GROUP_EDGES]))
-            grouped_tiles.append(grouped)
-
-        bias_ps = psum_acc.tile([P, LATENT], F32, name="acc")
-        nc.tensor.matmul(out=bias_ps[:], lhsT=ones[:], rhs=b_rows[:], start=True, stop=True)
-        bias_all = consts.tile([P, LATENT], F32)
-        nc.vector.tensor_copy(out=bias_all[:], in_=bias_ps[:])
+        table_warmer = consts.tile([P, 1], F32)
+        nc.scalar.activation(out=table_warmer[:], in_=ones[:, 0:1], func=RELU)
 
         w_grouped = consts.tile([P, LATENT, PACK], BF16, align_bytes=64)
         w_codes = consts.tile([P, LATENT], U32, align_bytes=64)
@@ -101,14 +89,22 @@ def tile_edgemodel_pa_kernel(tc, receiver, sender, edge_attr, global_attr, W1, b
                 in_=w_grouped[:, cols, :].rearrange("p n f -> p (n f)"),
             )
 
+        grouped_tiles = [
+            consts.tile([P, GROUP_EDGES, PACK], BF16, name="grouped%d" % n, align_bytes=64)
+            for n in range(GROUPED_TILES)
+        ]
+        bias_all = consts.tile([P, LATENT], F32)
         out_by_set = out.rearrange("(p t) n -> p t n", t=SETS)
         xt_of = {}
         codes_of = {}
         acc_of = {}
         y_of = {}
 
+        def planes_of(i):
+            return PACK if i < GROUPED_TILES else PIECES_PER_EDGE
+
         def transpose(i):
-            xt = psum_t.tile([P, PIECES_PER_EDGE, GROUP_EDGES], BF16, name="xt")
+            xt = psum_t.tile([P, PACK, GROUP_EDGES], BF16, name="xt")
             for j in range(GROUP_SETS):
                 for piece in range(PIECES_PER_EDGE):
                     nc.tensor.transpose(
@@ -116,13 +112,17 @@ def tile_edgemodel_pa_kernel(tc, receiver, sender, edge_attr, global_attr, W1, b
                         x_of_set[(piece, i * GROUP_SETS + j)],
                         ident[:],
                     )
+            if planes_of(i) == PACK:
+                nc.tensor.matmul(
+                    out=xt[:, PIECES_PER_EDGE, :], lhsT=g_rows[:], rhs=ones[:], start=True, stop=True
+                )
             xt_of[i] = xt
 
         def regroup(i):
-            grouped = grouped_tiles[i % GROUPED_TILES]
+            planes = planes_of(i)
             nc.scalar.copy(
-                out=grouped[:, :, 0:PIECES_PER_EDGE],
-                in_=xt_of[i][:].rearrange("p piece e -> p e piece"),
+                out=grouped_tiles[i % GROUPED_TILES][:, :, 0:planes],
+                in_=xt_of[i][:, 0:planes, :].rearrange("p f e -> p e f"),
             )
 
         def quantise(i):
@@ -152,32 +152,39 @@ def tile_edgemodel_pa_kernel(tc, receiver, sender, edge_attr, global_attr, W1, b
                 acc_of[(i, j)] = acc
 
         def add_bias(i):
+            y = y_pool.tile([P, GROUP_SETS, LATENT], F32, name="y")
             for j in range(GROUP_SETS):
-                y = y_pool.tile([P, LATENT], F32, name="y")
                 nc.vector.tensor_tensor(
-                    out=y[:], in0=acc_of[(i, j)][:], in1=bias_all[:], op=mybir.AluOpType.add
+                    out=y[:, j, :], in0=acc_of[(i, j)][:], in1=bias_all[:], op=mybir.AluOpType.add
                 )
-                y_of[(i, j)] = y
+            y_of[i] = y
 
         def relu_and_store(i):
-            y_scalar, y_gpsimd = y_of[(i, 0)], y_of[(i, 1)]
-            nc.scalar.activation(
-                out=y_scalar[:], in_=y_scalar[:], func=mybir.ActivationFunctionType.Relu
-            )
-            nc.sync.dma_start(out=out_by_set[:, i * GROUP_SETS, :], in_=y_scalar[:])
+            y = y_of[i]
+            nc.scalar.activation(out=y[:, 0, :], in_=y[:, 0, :], func=RELU)
             nc.gpsimd.tensor_scalar(
-                out=y_gpsimd[:],
-                in0=y_gpsimd[:],
+                out=y[:, 1, :],
+                in0=y[:, 1, :],
                 scalar1=float("inf"),
                 scalar2=0.0,
                 op0=mybir.AluOpType.min,
                 op1=mybir.AluOpType.max,
             )
-            nc.sync.dma_start(out=out_by_set[:, i * GROUP_SETS + 1, :], in_=y_gpsimd[:])
+            nc.sync.dma_start(
+                out=out_by_set[:, i * GROUP_SETS : (i + 1) * GROUP_SETS, :], in_=y[:]
+            )
 
         stages = (transpose, regroup, quantise, multiply, add_bias, relu_and_store)
-        for step in range(GROUPS + len(stages) - 1):
-            for lag, stage in enumerate(stages):
+
+        def run_step(step):
+            for lag in reversed(range(len(stages))):
                 i = step - lag
                 if 0 <= i < GROUPS:
-                    stage(i)
+                    stages[lag](i)
+
+        run_step(0)
+        bias_ps = psum_acc.tile([P, LATENT], F32, name="acc")
+        nc.tensor.matmul(out=bias_ps[:], lhsT=ones[:, 0:P], rhs=b_rows[:], start=True, stop=True)
+        nc.vector.tensor_copy(out=bias_all[:], in_=bias_ps[:])
+        for step in range(1, GROUPS + len(stages) - 1):
+            run_step(step)

@@ -19,8 +19,8 @@ LATENT = 512
 SETS = EDGES // P
 GROUP_SETS = 2
 GROUP_EDGES = GROUP_SETS * P
-GROUPS = SETS // GROUP_SETS
 GROUPED_TILES = 2
+GROUPS = [(0, 1), (1, 1)] + [(t, GROUP_SETS) for t in range(2, SETS, GROUP_SETS)]
 
 FLOPS = 2 * EDGES * (PACK * D_PIECE) * LATENT
 
@@ -43,7 +43,7 @@ def tile_edgemodel_pa_kernel(tc, receiver, sender, edge_attr, global_attr, W1, b
         consts = ctx.enter_context(tc.tile_pool(name="consts", bufs=1))
         x_pool = ctx.enter_context(tc.tile_pool(name="x", bufs=1))
         mx_pool = ctx.enter_context(tc.tile_pool(name="mx", bufs=3))
-        y_pool = ctx.enter_context(tc.tile_pool(name="y", bufs=6))
+        y_pool = ctx.enter_context(tc.tile_pool(name="y", bufs=12))
         psum_t = ctx.enter_context(tc.psum_pool(name="psum_t", bufs=3))
         psum_acc = ctx.enter_context(tc.psum_pool(name="psum_acc", bufs=5))
 
@@ -51,6 +51,8 @@ def tile_edgemodel_pa_kernel(tc, receiver, sender, edge_attr, global_attr, W1, b
         nc.vector.memset(g_rows[:], 0.0)
         b_rows = consts.tile([P, LATENT], BF16)
         nc.vector.memset(b_rows[:], 0.0)
+        nc.scalar.dma_start(out=g_rows[0:1, :], in_=global_attr)
+        nc.scalar.dma_start(out=b_rows[0:1, :], in_=b1.rearrange("(o n) -> o n", o=1))
         ones = consts.tile([P, GROUP_EDGES], BF16)
         nc.vector.memset(ones[:], 1.0)
         ident = consts.tile([P, P], BF16)
@@ -67,9 +69,6 @@ def tile_edgemodel_pa_kernel(tc, receiver, sender, edge_attr, global_attr, W1, b
                 nc.sync.dma_start(out=chunk[:], in_=by_set[:, first : first + width, :])
                 for k in range(width):
                     x_of_set[(piece, first + k)] = chunk[:, k, :]
-            if first == 0:
-                nc.scalar.dma_start(out=g_rows[0:1, :], in_=global_attr)
-                nc.scalar.dma_start(out=b_rows[0:1, :], in_=b1.rearrange("(o n) -> o n", o=1))
 
         table_warmer = consts.tile([P, 1], F32)
         nc.scalar.activation(out=table_warmer[:], in_=ones[:, 0:1], func=RELU)
@@ -78,10 +77,13 @@ def tile_edgemodel_pa_kernel(tc, receiver, sender, edge_attr, global_attr, W1, b
         w_codes = consts.tile([P, LATENT], U32, align_bytes=64)
         w_scales = consts.tile([P, LATENT], U8, align_bytes=64)
         w_halves = (slice(0, LATENT // 2), slice(LATENT // 2, LATENT))
-        for cols in w_halves:
-            nc.vector.tensor_copy(
-                out=w_grouped[:, cols, :], in_=w_raw[:, :, cols].rearrange("p f n -> p n f")
-            )
+        w_parts = (
+            (nc.vector.tensor_copy, slice(0, LATENT // 2)),
+            (nc.scalar.copy, slice(3 * LATENT // 4, LATENT)),
+            (nc.vector.tensor_copy, slice(LATENT // 2, 3 * LATENT // 4)),
+        )
+        for copy, cols in w_parts:
+            copy(out=w_grouped[:, cols, :], in_=w_raw[:, :, cols].rearrange("p f n -> p n f"))
         for cols in w_halves:
             nc.vector.quantize_mx(
                 out=w_codes[:, cols].bitcast(FP8X4),
@@ -99,45 +101,53 @@ def tile_edgemodel_pa_kernel(tc, receiver, sender, edge_attr, global_attr, W1, b
         codes_of = {}
         acc_of = {}
         y_of = {}
-
-        def planes_of(i):
-            return PACK if i < GROUPED_TILES else PIECES_PER_EDGE
+        planes_of = []
+        places_filled = set()
+        for i, (first, width) in enumerate(GROUPS):
+            places = {(i % GROUPED_TILES, j) for j in range(width)}
+            planes_of.append(PIECES_PER_EDGE if places <= places_filled else PACK)
+            places_filled = places_filled | places
 
         def transpose(i):
+            first, width = GROUPS[i]
             xt = psum_t.tile([P, PACK, GROUP_EDGES], BF16, name="xt")
-            for j in range(GROUP_SETS):
+            if planes_of[i] == PACK:
+                nc.tensor.matmul(
+                    out=xt[:, PIECES_PER_EDGE, 0 : width * P],
+                    lhsT=g_rows[:],
+                    rhs=ones[:, 0 : width * P],
+                    start=True,
+                    stop=True,
+                )
+            for j in range(width):
                 for piece in range(PIECES_PER_EDGE):
                     nc.tensor.transpose(
-                        xt[:, piece, j * P : (j + 1) * P],
-                        x_of_set[(piece, i * GROUP_SETS + j)],
-                        ident[:],
+                        xt[:, piece, j * P : (j + 1) * P], x_of_set[(piece, first + j)], ident[:]
                     )
-            if planes_of(i) == PACK:
-                nc.tensor.matmul(
-                    out=xt[:, PIECES_PER_EDGE, :], lhsT=g_rows[:], rhs=ones[:], start=True, stop=True
-                )
             xt_of[i] = xt
 
         def regroup(i):
-            planes = planes_of(i)
+            planes = planes_of[i]
+            edges = GROUPS[i][1] * P
             nc.scalar.copy(
-                out=grouped_tiles[i % GROUPED_TILES][:, :, 0:planes],
-                in_=xt_of[i][:, 0:planes, :].rearrange("p f e -> p e f"),
+                out=grouped_tiles[i % GROUPED_TILES][:, 0:edges, 0:planes],
+                in_=xt_of[i][:, 0:planes, 0:edges].rearrange("p f e -> p e f"),
             )
 
         def quantise(i):
+            edges = GROUPS[i][1] * P
             codes = mx_pool.tile([P, GROUP_EDGES], U32, name="x_codes", align_bytes=64)
             scales = mx_pool.tile([P, GROUP_EDGES], U8, name="x_scales", align_bytes=64)
             nc.vector.quantize_mx(
-                out=codes[:].bitcast(FP8X4),
-                scales=scales[:],
-                in_=grouped_tiles[i % GROUPED_TILES][:].rearrange("p e f -> p (e f)"),
+                out=codes[:, 0:edges].bitcast(FP8X4),
+                scales=scales[:, 0:edges],
+                in_=grouped_tiles[i % GROUPED_TILES][:, 0:edges, :].rearrange("p e f -> p (e f)"),
             )
             codes_of[i] = (codes, scales)
 
         def multiply(i):
             codes, scales = codes_of[i]
-            for j in range(GROUP_SETS):
+            for j in range(GROUPS[i][1]):
                 edges = slice(j * P, (j + 1) * P)
                 acc = psum_acc.tile([P, LATENT], F32, name="acc")
                 nc.tensor.matmul_mx(
@@ -153,38 +163,49 @@ def tile_edgemodel_pa_kernel(tc, receiver, sender, edge_attr, global_attr, W1, b
 
         def add_bias(i):
             y = y_pool.tile([P, GROUP_SETS, LATENT], F32, name="y")
-            for j in range(GROUP_SETS):
+            for j in range(GROUPS[i][1]):
                 nc.vector.tensor_tensor(
                     out=y[:, j, :], in0=acc_of[(i, j)][:], in1=bias_all[:], op=mybir.AluOpType.add
                 )
             y_of[i] = y
 
-        def relu_and_store(i):
-            y = y_of[i]
-            nc.scalar.activation(out=y[:, 0, :], in_=y[:, 0, :], func=RELU)
+        def relu_on_scalar(y_part):
+            nc.scalar.activation(out=y_part, in_=y_part, func=RELU)
+
+        def relu_on_gpsimd(y_part):
             nc.gpsimd.tensor_scalar(
-                out=y[:, 1, :],
-                in0=y[:, 1, :],
+                out=y_part,
+                in0=y_part,
                 scalar1=float("inf"),
                 scalar2=0.0,
                 op0=mybir.AluOpType.min,
                 op1=mybir.AluOpType.max,
             )
-            nc.sync.dma_start(
-                out=out_by_set[:, i * GROUP_SETS : (i + 1) * GROUP_SETS, :], in_=y[:]
-            )
+
+        def relu_and_store(i):
+            first, width = GROUPS[i]
+            y = y_of[i]
+            if width == GROUP_SETS:
+                relu_on_scalar(y[:, 0, :])
+                relu_on_gpsimd(y[:, 1, :])
+            else:
+                relu_on_scalar(y[:, 0, 0 : LATENT // 2])
+                relu_on_gpsimd(y[:, 0, LATENT // 2 : LATENT])
+            nc.sync.dma_start(out=out_by_set[:, first : first + width, :], in_=y[:, 0:width, :])
 
         stages = (transpose, regroup, quantise, multiply, add_bias, relu_and_store)
 
         def run_step(step):
             for lag in reversed(range(len(stages))):
                 i = step - lag
-                if 0 <= i < GROUPS:
+                if 0 <= i < len(GROUPS):
                     stages[lag](i)
 
         run_step(0)
+        run_step(1)
         bias_ps = psum_acc.tile([P, LATENT], F32, name="acc")
         nc.tensor.matmul(out=bias_ps[:], lhsT=ones[:, 0:P], rhs=b_rows[:], start=True, stop=True)
+        run_step(2)
         nc.vector.tensor_copy(out=bias_all[:], in_=bias_ps[:])
-        for step in range(1, GROUPS + len(stages) - 1):
+        for step in range(3, len(GROUPS) + len(stages) - 1):
             run_step(step)

@@ -22,6 +22,8 @@ GROUP_EDGES = GROUP_SETS * P
 GROUPED_TILES = 2
 GROUPS = [(0, 1), (1, 1)] + [(t, GROUP_SETS) for t in range(2, SETS, GROUP_SETS)]
 
+GPSIMD_WHOLE_GROUP = 3
+
 FLOPS = 2 * EDGES * (PACK * D_PIECE) * LATENT
 
 
@@ -111,6 +113,11 @@ def tile_edgemodel_pa_kernel(tc, receiver, sender, edge_attr, global_attr, W1, b
         def transpose(i):
             first, width = GROUPS[i]
             xt = psum_t.tile([P, PACK, GROUP_EDGES], BF16, name="xt")
+            for j in range(width):
+                for piece in range(PIECES_PER_EDGE):
+                    nc.tensor.transpose(
+                        xt[:, piece, j * P : (j + 1) * P], x_of_set[(piece, first + j)], ident[:]
+                    )
             if planes_of[i] == PACK:
                 nc.tensor.matmul(
                     out=xt[:, PIECES_PER_EDGE, 0 : width * P],
@@ -119,11 +126,6 @@ def tile_edgemodel_pa_kernel(tc, receiver, sender, edge_attr, global_attr, W1, b
                     start=True,
                     stop=True,
                 )
-            for j in range(width):
-                for piece in range(PIECES_PER_EDGE):
-                    nc.tensor.transpose(
-                        xt[:, piece, j * P : (j + 1) * P], x_of_set[(piece, first + j)], ident[:]
-                    )
             xt_of[i] = xt
 
         def regroup(i):
@@ -186,7 +188,10 @@ def tile_edgemodel_pa_kernel(tc, receiver, sender, edge_attr, global_attr, W1, b
             first, width = GROUPS[i]
             y = y_of[i]
             if width == GROUP_SETS:
-                relu_on_scalar(y[:, 0, :])
+                if i % GPSIMD_WHOLE_GROUP == 0:
+                    relu_on_gpsimd(y[:, 0, :])
+                else:
+                    relu_on_scalar(y[:, 0, :])
                 relu_on_gpsimd(y[:, 1, :])
             else:
                 relu_on_scalar(y[:, 0, 0 : LATENT // 2])

@@ -22,8 +22,6 @@ GROUP_EDGES = GROUP_SETS * P
 GROUPED_TILES = 2
 GROUPS = [(0, 1), (1, 1)] + [(t, GROUP_SETS) for t in range(2, SETS, GROUP_SETS)]
 
-GPSIMD_WHOLE_GROUP = 3
-
 FLOPS = 2 * EDGES * (PACK * D_PIECE) * LATENT
 
 
@@ -167,7 +165,7 @@ def tile_edgemodel_pa_kernel(tc, receiver, sender, edge_attr, global_attr, W1, b
             y = y_pool.tile([P, GROUP_SETS, LATENT], F32, name="y")
             for j in range(GROUPS[i][1]):
                 nc.vector.tensor_tensor(
-                    out=y[:, j, :], in0=acc_of[(i, j)][:], in1=bias_all[:], op=mybir.AluOpType.add
+                    out=y[:, j, :], in0=bias_all[:], in1=acc_of[(i, j)][:], op=mybir.AluOpType.add
                 )
             y_of[i] = y
 
@@ -188,10 +186,7 @@ def tile_edgemodel_pa_kernel(tc, receiver, sender, edge_attr, global_attr, W1, b
             first, width = GROUPS[i]
             y = y_of[i]
             if width == GROUP_SETS:
-                if i % GPSIMD_WHOLE_GROUP == 0:
-                    relu_on_gpsimd(y[:, 0, :])
-                else:
-                    relu_on_scalar(y[:, 0, :])
+                relu_on_scalar(y[:, 0, :])
                 relu_on_gpsimd(y[:, 1, :])
             else:
                 relu_on_scalar(y[:, 0, 0 : LATENT // 2])

@@ -19,8 +19,14 @@ LATENT = 512
 SETS = EDGES // P
 GROUP_SETS = 2
 GROUP_EDGES = GROUP_SETS * P
-GROUPED_TILES = 2
-GROUPS = [(0, 1), (1, 1)] + [(t, GROUP_SETS) for t in range(2, SETS, GROUP_SETS)]
+GROUPED_TILES = 3
+GROUPS = (
+    [(0, 1), (1, 1)]
+    + [(t, GROUP_SETS) for t in range(2, SETS - 2, GROUP_SETS)]
+    + [(SETS - 2, 1), (SETS - 1, 1)]
+)
+VECTOR_W_COLUMNS = 176
+WARMUP_MATMULS = 2
 
 FLOPS = 2 * EDGES * (PACK * D_PIECE) * LATENT
 
@@ -28,7 +34,7 @@ FLOPS = 2 * EDGES * (PACK * D_PIECE) * LATENT
 def load_chunks():
     chunks = []
     first = 0
-    width = 2 * GROUP_SETS
+    width = GROUP_SETS
     while first < SETS:
         chunks.append((first, width))
         first += width
@@ -51,15 +57,21 @@ def tile_edgemodel_pa_kernel(tc, receiver, sender, edge_attr, global_attr, W1, b
         nc.vector.memset(g_rows[:], 0.0)
         b_rows = consts.tile([P, LATENT], BF16)
         nc.vector.memset(b_rows[:], 0.0)
-        nc.scalar.dma_start(out=g_rows[0:1, :], in_=global_attr)
-        nc.scalar.dma_start(out=b_rows[0:1, :], in_=b1.rearrange("(o n) -> o n", o=1))
+        warmup = consts.tile([P, LATENT], BF16)
+        nc.vector.memset(warmup[:], 0.0)
         ones = consts.tile([P, GROUP_EDGES], BF16)
         nc.vector.memset(ones[:], 1.0)
         ident = consts.tile([P, P], BF16)
         masks.make_identity(nc, ident[:])
 
-        w_raw = consts.tile([P, PACK, LATENT], BF16)
-        nc.sync.dma_start(out=w_raw[:], in_=W1.rearrange("(f p) n -> p f n", p=P))
+        half = LATENT // 2
+        w_by_partition = W1.rearrange("(f p) n -> p f n", p=P)
+        w_raw = [consts.tile([P, PACK, half], BF16, name="w_raw%d" % h) for h in range(2)]
+
+        def load_w(h):
+            nc.sync.dma_start(out=w_raw[h][:], in_=w_by_partition[:, :, h * half : (h + 1) * half])
+
+        load_w(0)
 
         x_of_set = {}
         for first, width in load_chunks():
@@ -69,6 +81,10 @@ def tile_edgemodel_pa_kernel(tc, receiver, sender, edge_attr, global_attr, W1, b
                 nc.sync.dma_start(out=chunk[:], in_=by_set[:, first : first + width, :])
                 for k in range(width):
                     x_of_set[(piece, first + k)] = chunk[:, k, :]
+            if first == 0:
+                nc.sync.dma_start(out=g_rows[0:1, :], in_=global_attr)
+                load_w(1)
+                nc.sync.dma_start(out=b_rows[0:1, :], in_=b1.rearrange("(o n) -> o n", o=1))
 
         table_warmer = consts.tile([P, 1], F32)
         nc.scalar.activation(out=table_warmer[:], in_=ones[:, 0:1], func=RELU)
@@ -76,15 +92,15 @@ def tile_edgemodel_pa_kernel(tc, receiver, sender, edge_attr, global_attr, W1, b
         w_grouped = consts.tile([P, LATENT, PACK], BF16, align_bytes=64)
         w_codes = consts.tile([P, LATENT], U32, align_bytes=64)
         w_scales = consts.tile([P, LATENT], U8, align_bytes=64)
-        w_halves = (slice(0, LATENT // 2), slice(LATENT // 2, LATENT))
-        w_parts = (
-            (nc.vector.tensor_copy, slice(0, LATENT // 2)),
-            (nc.scalar.copy, slice(3 * LATENT // 4, LATENT)),
-            (nc.vector.tensor_copy, slice(LATENT // 2, 3 * LATENT // 4)),
-        )
-        for copy, cols in w_parts:
-            copy(out=w_grouped[:, cols, :], in_=w_raw[:, :, cols].rearrange("p f n -> p n f"))
-        for cols in w_halves:
+
+        def regroup_w(copy, h, first, last):
+            copy(
+                out=w_grouped[:, h * half + first : h * half + last, :],
+                in_=w_raw[h][:, :, first:last].rearrange("p f n -> p n f"),
+            )
+
+        def quantise_w(h):
+            cols = slice(h * half, (h + 1) * half)
             nc.vector.quantize_mx(
                 out=w_codes[:, cols].bitcast(FP8X4),
                 scales=w_scales[:, cols],
@@ -161,12 +177,21 @@ def tile_edgemodel_pa_kernel(tc, receiver, sender, edge_attr, global_attr, W1, b
                 )
                 acc_of[(i, j)] = acc
 
+        def column_parts(i):
+            whole = [slice(0, LATENT)]
+            halves = [slice(0, LATENT // 2), slice(LATENT // 2, LATENT)]
+            return halves if i == len(GROUPS) - 1 else whole
+
         def add_bias(i):
             y = y_pool.tile([P, GROUP_SETS, LATENT], F32, name="y")
             for j in range(GROUPS[i][1]):
-                nc.vector.tensor_tensor(
-                    out=y[:, j, :], in0=bias_all[:], in1=acc_of[(i, j)][:], op=mybir.AluOpType.add
-                )
+                for cols in column_parts(i):
+                    nc.vector.tensor_tensor(
+                        out=y[:, j, cols],
+                        in0=acc_of[(i, j)][:, cols],
+                        in1=bias_all[:, cols],
+                        op=mybir.AluOpType.add,
+                    )
             y_of[i] = y
 
         def relu_on_scalar(y_part):
@@ -188,10 +213,15 @@ def tile_edgemodel_pa_kernel(tc, receiver, sender, edge_attr, global_attr, W1, b
             if width == GROUP_SETS:
                 relu_on_scalar(y[:, 0, :])
                 relu_on_gpsimd(y[:, 1, :])
-            else:
+            elif i < len(GROUPS) - 1:
                 relu_on_scalar(y[:, 0, 0 : LATENT // 2])
                 relu_on_gpsimd(y[:, 0, LATENT // 2 : LATENT])
-            nc.sync.dma_start(out=out_by_set[:, first : first + width, :], in_=y[:, 0:width, :])
+            for cols in column_parts(i):
+                if i == len(GROUPS) - 1:
+                    relu_on_scalar(y[:, 0, cols])
+                nc.sync.dma_start(
+                    out=out_by_set[:, first : first + width, cols], in_=y[:, 0:width, cols]
+                )
 
         stages = (transpose, regroup, quantise, multiply, add_bias, relu_and_store)
 
@@ -201,11 +231,18 @@ def tile_edgemodel_pa_kernel(tc, receiver, sender, edge_attr, global_attr, W1, b
                 if 0 <= i < len(GROUPS):
                     stages[lag](i)
 
+        bias_ps = psum_acc.tile([P, LATENT], F32, name="acc")
+        for n in range(WARMUP_MATMULS):
+            nc.tensor.matmul(out=bias_ps[:], lhsT=warmup[:, 0:P], rhs=warmup[:], start=True, stop=True)
+        regroup_w(nc.vector.tensor_copy, 0, 0, VECTOR_W_COLUMNS)
+        regroup_w(nc.scalar.copy, 0, VECTOR_W_COLUMNS, half)
+        quantise_w(0)
         run_step(0)
         run_step(1)
-        bias_ps = psum_acc.tile([P, LATENT], F32, name="acc")
         nc.tensor.matmul(out=bias_ps[:], lhsT=ones[:, 0:P], rhs=b_rows[:], start=True, stop=True)
+        regroup_w(nc.vector.tensor_copy, 1, 0, half)
         run_step(2)
+        quantise_w(1)
         nc.vector.tensor_copy(out=bias_all[:], in_=bias_ps[:])
         for step in range(3, len(GROUPS) + len(stages) - 1):
             run_step(step)

from contextlib import ExitStack

import concourse.masks as masks
import concourse.mybir as mybir

FP8X4 = mybir.dt.float8_e4m3fn_x4
BF16 = mybir.dt.bfloat16
F32 = mybir.dt.float32
U32 = mybir.dt.uint32
U8 = mybir.dt.uint8
RELU = mybir.ActivationFunctionType.Relu

P = 128
PACK = 4
EDGES = 4096
D_PIECE = 128
PIECES_PER_EDGE = 3
LATENT = 512
SETS = EDGES // P
GROUP_SETS = 2
GROUP_EDGES = GROUP_SETS * P
GROUPED_TILES = 3
GROUPS = (
    [(0, 1), (1, 1)]
    + [(t, GROUP_SETS) for t in range(2, SETS - 2, GROUP_SETS)]
    + [(SETS - 2, 1), (SETS - 1, 1)]
)
VECTOR_W_COLUMNS = 176
WARMUP_MATMULS = 2

FLOPS = 2 * EDGES * (PACK * D_PIECE) * LATENT


def load_chunks():
    chunks = []
    first = 0
    width = GROUP_SETS
    while first < SETS:
        chunks.append((first, width))
        first += width
        width = first
    return chunks


def tile_edgemodel_pa_kernel(tc, receiver, sender, edge_attr, global_attr, W1, b1, out):
    nc = tc.nc
    with ExitStack() as ctx:
        ctx.enter_context(tc.manual_schedule())
        consts = ctx.enter_context(tc.tile_pool(name="consts", bufs=1))
        x_pool = ctx.enter_context(tc.tile_pool(name="x", bufs=1))
        mx_pool = ctx.enter_context(tc.tile_pool(name="mx", bufs=3))
        y_pool = ctx.enter_context(tc.tile_pool(name="y", bufs=12))
        psum_t = ctx.enter_context(tc.psum_pool(name="psum_t", bufs=3))
        psum_acc = ctx.enter_context(tc.psum_pool(name="psum_acc", bufs=5))

        g_rows = consts.tile([P, D_PIECE], BF16)
        nc.vector.memset(g_rows[:], 0.0)
        b_rows = consts.tile([P, LATENT], BF16)
        nc.vector.memset(b_rows[:], 0.0)
        warmup = consts.tile([P, LATENT], BF16)
        nc.vector.memset(warmup[:], 0.0)
        ones = consts.tile([P, GROUP_EDGES], BF16)
        nc.vector.memset(ones[:], 1.0)
        ident = consts.tile([P, P], BF16)
        masks.make_identity(nc, ident[:])

        half = LATENT // 2
        w_by_partition = W1.rearrange("(f p) n -> p f n", p=P)
        w_raw = [consts.tile([P, PACK, half], BF16, name="w_raw%d" % h) for h in range(2)]

        def load_w(h):
            nc.sync.dma_start(out=w_raw[h][:], in_=w_by_partition[:, :, h * half : (h + 1) * half])

        load_w(0)

        x_of_set = {}
        for first, width in load_chunks():
            for piece, source in enumerate((receiver, sender, edge_attr)):
                chunk = x_pool.tile([P, width, D_PIECE], BF16, name="x%d_%d" % (piece, first))
                by_set = source.rearrange("(p t) d -> p t d", t=SETS)
                nc.sync.dma_start(out=chunk[:], in_=by_set[:, first : first + width, :])
                for k in range(width):
                    x_of_set[(piece, first + k)] = chunk[:, k, :]
            if first == 0:
                nc.sync.dma_start(out=g_rows[0:1, :], in_=global_attr)
                load_w(1)
                nc.sync.dma_start(out=b_rows[0:1, :], in_=b1.rearrange("(o n) -> o n", o=1))

        table_warmer = consts.tile([P, 1], F32)
        nc.scalar.activation(out=table_warmer[:], in_=ones[:, 0:1], func=RELU)

        w_grouped = consts.tile([P, LATENT, PACK], BF16, align_bytes=64)
        w_codes = consts.tile([P, LATENT], U32, align_bytes=64)
        w_scales = consts.tile([P, LATENT], U8, align_bytes=64)

        def regroup_w(copy, h, first, last):
            copy(
                out=w_grouped[:, h * half + first : h * half + last, :],
                in_=w_raw[h][:, :, first:last].rearrange("p f n -> p n f"),
            )

        def quantise_w(h):
            cols = slice(h * half, (h + 1) * half)
            nc.vector.quantize_mx(
                out=w_codes[:, cols].bitcast(FP8X4),
                scales=w_scales[:, cols],
                in_=w_grouped[:, cols, :].rearrange("p n f -> p (n f)"),
            )

        grouped_tiles = [
            consts.tile([P, GROUP_EDGES, PACK], BF16, name="grouped%d" % n, align_bytes=64)
            for n in range(GROUPED_TILES)
        ]
        bias_all = consts.tile([P, LATENT], F32)
        out_by_set = out.rearrange("(p t) n -> p t n", t=SETS)
        xt_of = {}
        codes_of = {}
        acc_of = {}
        y_of = {}
        planes_of = []
        places_filled = set()
        for i, (first, width) in enumerate(GROUPS):
            places = {(i % GROUPED_TILES, j) for j in range(width)}
            planes_of.append(PIECES_PER_EDGE if places <= places_filled else PACK)
            places_filled = places_filled | places

        def transpose(i):
            first, width = GROUPS[i]
            xt = psum_t.tile([P, PACK, GROUP_EDGES], BF16, name="xt")
            for j in range(width):
                for piece in range(PIECES_PER_EDGE):
                    nc.tensor.transpose(
                        xt[:, piece, j * P : (j + 1) * P], x_of_set[(piece, first + j)], ident[:]
                    )
            if planes_of[i] == PACK:
                nc.tensor.matmul(
                    out=xt[:, PIECES_PER_EDGE, 0 : width * P],
                    lhsT=g_rows[:],
                    rhs=ones[:, 0 : width * P],
                    start=True,
                    stop=True,
                )
            xt_of[i] = xt

        def regroup(i):
            planes = planes_of[i]
            edges = GROUPS[i][1] * P
            nc.scalar.copy(
                out=grouped_tiles[i % GROUPED_TILES][:, 0:edges, 0:planes],
                in_=xt_of[i][:, 0:planes, 0:edges].rearrange("p f e -> p e f"),
            )

        def quantise(i):
            edges = GROUPS[i][1] * P
            codes = mx_pool.tile([P, GROUP_EDGES], U32, name="x_codes", align_bytes=64)
            scales = mx_pool.tile([P, GROUP_EDGES], U8, name="x_scales", align_bytes=64)
            nc.vector.quantize_mx(
                out=codes[:, 0:edges].bitcast(FP8X4),
                scales=scales[:, 0:edges],
                in_=grouped_tiles[i % GROUPED_TILES][:, 0:edges, :].rearrange("p e f -> p (e f)"),
            )
            codes_of[i] = (codes, scales)

        def multiply(i):
            codes, scales = codes_of[i]
            for j in range(GROUPS[i][1]):
                edges = slice(j * P, (j + 1) * P)
                acc = psum_acc.tile([P, LATENT], F32, name="acc")
                nc.tensor.matmul_mx(
                    out=acc[:],
                    lhsT=codes[:, edges].bitcast(FP8X4),
                    lhsT_scale=scales[:, edges],
                    rhs=w_codes[:].bitcast(FP8X4),
                    rhs_scale=w_scales[:],
                    start=True,
                    stop=True,
                )
                acc_of[(i, j)] = acc

        def column_parts(i):
            whole = [slice(0, LATENT)]
            halves = [slice(0, LATENT // 2), slice(LATENT // 2, LATENT)]
            return halves if i == len(GROUPS) - 1 else whole

        def add_bias(i):
            y = y_pool.tile([P, GROUP_SETS, LATENT], F32, name="y")
            for j in range(GROUPS[i][1]):
                for cols in column_parts(i):
                    nc.vector.tensor_tensor(
                        out=y[:, j, cols],
                        in0=acc_of[(i, j)][:, cols],
                        in1=bias_all[:, cols],
                        op=mybir.AluOpType.add,
                    )
            y_of[i] = y

        def relu_on_scalar(y_part):
            nc.scalar.activation(out=y_part, in_=y_part, func=RELU)

        def relu_on_gpsimd(y_part):
            nc.gpsimd.tensor_scalar(
                out=y_part,
                in0=y_part,
                scalar1=float("inf"),
                scalar2=0.0,
                op0=mybir.AluOpType.min,
                op1=mybir.AluOpType.max,
            )

        def relu_and_store(i):
            first, width = GROUPS[i]
            y = y_of[i]
            if width == GROUP_SETS:
                relu_on_scalar(y[:, 0, :])
                relu_on_gpsimd(y[:, 1, :])
            elif i < len(GROUPS) - 1:
                relu_on_scalar(y[:, 0, 0 : LATENT // 2])
                relu_on_gpsimd(y[:, 0, LATENT // 2 : LATENT])
            for cols in column_parts(i):
                if i == len(GROUPS) - 1:
                    relu_on_scalar(y[:, 0, cols])
                nc.sync.dma_start(
                    out=out_by_set[:, first : first + width, cols], in_=y[:, 0:width, cols]
                )

        stages = (transpose, regroup, quantise, multiply, add_bias, relu_and_store)

        def run_step(step):
            for lag in reversed(range(len(stages))):
                i = step - lag
                if 0 <= i < len(GROUPS):
                    stages[lag](i)

        bias_ps = psum_acc.tile([P, LATENT], F32, name="acc")
        for n in range(WARMUP_MATMULS):
            nc.tensor.matmul(out=bias_ps[:], lhsT=warmup[:, 0:P], rhs=warmup[:], start=True, stop=True)
        regroup_w(nc.vector.tensor_copy, 0, 0, VECTOR_W_COLUMNS)
        regroup_w(nc.scalar.copy, 0, VECTOR_W_COLUMNS, half)
        quantise_w(0)
        run_step(0)
        run_step(1)
        nc.tensor.matmul(out=bias_ps[:], lhsT=ones[:, 0:P], rhs=b_rows[:], start=True, stop=True)
        regroup_w(nc.vector.tensor_copy, 1, 0, half)
        run_step(2)
        quantise_w(1)
        nc.vector.tensor_copy(out=bias_all[:], in_=bias_ps[:])
        for step in range(3, len(GROUPS) + len(stages) - 1):
            run_step(step)
